import numpy as np
import ml_dtypes


def mxq(x, axis, fmt="e4m3"):
    dtype, down = {"e4m3": (ml_dtypes.float8_e4m3fn, 7), "e5m2": (ml_dtypes.float8_e5m2, 14)}[fmt]
    v = np.moveaxis(np.asarray(x, np.float32).astype(ml_dtypes.bfloat16).astype(np.float64), axis, -1)
    blocks = v.reshape(v.shape[:-1] + (-1, 32))
    amax = np.abs(blocks).max(-1, keepdims=True)
    byte = np.maximum(np.where(amax > 0, np.frexp(amax)[1] - 1 + 127, 0) - down, 1)
    scale = np.exp2(byte - 127.0)
    codes = (blocks / scale).astype(np.float32).astype(dtype).astype(np.float64)
    return np.moveaxis((codes * scale).reshape(v.shape), -1, axis)


WIDE = False


def mx_kscale(k):
    if not WIDE:
        return np.ones(k)
    levels = np.array([10, -10, 5, -5, 0])
    if k % 512:
        return np.exp2(np.random.permutation(np.resize(levels, k // 32))).repeat(32)
    a = np.empty((k // 512, 16))
    for p in range(k // 512):
        a[p, :8] = np.random.permutation(np.resize(levels, 8))
        for g in range(8):
            far = levels[np.abs(levels - a[p, g]) >= 10]
            a[p, g + 8] = far[np.random.randint(len(far))]
    return np.exp2(a.ravel()).repeat(32)


BF16 = ml_dtypes.bfloat16


def bf(x):
    return np.asarray(x, np.float32).astype(BF16)


def f64(x):
    return np.asarray(x).astype(np.float64)


N, M, D, K = 1024, 1024, 512, 3
SLOPE = 0.01


def leaky_relu(v):
    return np.where(v >= 0.0, v, SLOPE * v)


def setup_inputs():
    s, t = mx_kscale(D), mx_kscale(D)
    return {"p_last": bf(leaky_relu(np.random.standard_normal((M, D)) * 0.3 - 0.1) * s),
            "q_last": bf(leaky_relu(np.random.standard_normal((N, D)) * 0.3 - 0.1) / t),
            "distance_matrix": bf(np.random.uniform(size=(M, N)) + 0.1),
            "Wd": bf(np.random.standard_normal((D, D)) / np.sqrt(D) * t[:, None] / s[None, :]),
            "bd": bf(np.random.standard_normal(D) * 0.1 * t),
            "a": bf(np.random.uniform(0.5, 1.0, size=(1,))),
            "b": bf(-np.random.uniform(0.5, 1.0, size=(1,))),
            "c": bf(-np.random.uniform(0.5, 1.0, size=(1,)))}


def reference(p_last, q_last, distance_matrix, Wd, bd, a, b, c):
    dist = f64(distance_matrix)
    fx = f64(a)[0] * dist ** f64(b)[0] * np.exp(f64(c)[0] * dist)
    dec = (mxq(f64(p_last), 1, "e4m3") @ mxq(f64(Wd).T, 0, "e4m3")) + f64(bd)
    return (mxq(dec, 1, "e4m3") @ mxq(f64(q_last).T, 0, "e4m3")) * fx

@@ -1,0 +1,314 @@
+from contextlib import ExitStack
+
+import concourse.mybir as mybir
+from concourse.masks import make_identity
+
+FLOPS = 2 * 1024 * 512 * 512 + 2 * 1024 * 1024 * 512
+
+F32 = mybir.dt.float32
+BF16 = mybir.dt.bfloat16
+U32 = mybir.dt.uint32
+U8 = mybir.dt.uint8
+FP8X4 = mybir.dt.float8_e4m3fn_x4
+ACT = mybir.ActivationFunctionType
+ALU = mybir.AluOpType
+
+P = 128
+G = 8
+N = 1024
+D = 512
+BANK_DT = F32
+V_COPIES = ()
+
+
+def tile_gglr_pb_kernel(tc, p_last, q_last, distance_matrix, Wd, bd, a, b, c, out):
+    nc = tc.nc
+    with ExitStack() as ctx:
+        ctx.enter_context(tc.manual_schedule())
+        sb = ctx.enter_context(tc.tile_pool(name="sb", bufs=1))
+        trp = ctx.enter_context(tc.psum_pool(name="trp", bufs=3))
+        s1p = ctx.enter_context(tc.psum_pool(name="s1p", bufs=2))
+        s2p = ctx.enter_context(tc.psum_pool(name="s2p", bufs=3))
+
+        d_v = distance_matrix.rearrange("(r g) n -> r g n", g=G)
+        o_v = out.rearrange("(r g) n -> r g n", g=G)
+        p_v = p_last.rearrange("(r g) k -> r g k", g=G)
+        q_v = q_last.rearrange("(h r) k -> r h k", r=P)
+        w_v = Wd.rearrange("(s q) k -> s q k", q=4)
+
+        c_bf = sb.tile([P, 1], BF16, name="c_bf")
+        b_bf = sb.tile([P, 1], BF16, name="b_bf")
+        a_bf = sb.tile([P, 1], BF16, name="a_bf")
+        one1 = sb.tile([P, 1], F32, name="one1")
+        junk = sb.tile([P, 1], F32, name="junk")
+        c_sq = sb.tile([P, 1], F32, name="c_sq")
+        c_fix = sb.tile([P, 1], F32, name="c_fix")
+        c_safe = sb.tile([P, 1], F32, name="c_safe")
+        c_inv = sb.tile([P, 1], F32, name="c_inv")
+        ratio = sb.tile([P, 1], F32, name="ratio")
+        ident = sb.tile([P, P], F32, name="ident")
+        ones = sb.tile([P, P], BF16, name="ones")
+        bd_row = sb.tile([P, D], BF16, name="bd_row")
+        bias_bc = sb.tile([P, D], BF16, name="bias_bc")
+
+        d_sb = [sb.tile([P, N], BF16, name="d_sb%d" % g) for g in range(G)]
+        ln_sb = [sb.tile([P, N], F32, name="ln_sb%d" % g) for g in range(G)]
+        fx_sb = [sb.tile([P, N], F32, name="fx_sb%d" % g) for g in range(G)]
+        o_sb = [sb.tile([P, N], F32, name="o_sb%d" % g) for g in range(G)]
+
+        w_sb = sb.tile([P, 4, D], BF16, name="w_sb")
+        p_sb = [sb.tile([P, 2, D], BF16, name="p_sb%d" % j) for j in range(4)]
+        q_sb = [sb.tile([P, 2, D], BF16, name="q_sb%d" % j) for j in range(4)]
+        w_g = sb.tile([P, 4 * D], BF16, name="w_g", align_bytes=64)
+        p_g = [sb.tile([P, 4 * D], BF16, name="p_g%d" % h, align_bytes=64) for h in range(2)]
+        q_g = [sb.tile([P, 4 * D], BF16, name="q_g%d" % h, align_bytes=64) for h in range(2)]
+        dec_sb = [sb.tile([P, D], BF16, name="dec_sb%d" % g) for g in range(G)]
+        dec_g = [sb.tile([P, 2 * D], BF16, name="dec_g%d" % j, align_bytes=64) for j in range(4)]
+        w_c = sb.tile([P, D], U32, name="w_c", align_bytes=64)
+        w_s = sb.tile([P, D], U8, name="w_s", align_bytes=64)
+        p_c = [sb.tile([P, D], U32, name="p_c%d" % h, align_bytes=64) for h in range(2)]
+        p_s = [sb.tile([P, D], U8, name="p_s%d" % h, align_bytes=64) for h in range(2)]
+        q_c = [sb.tile([P, D], U32, name="q_c%d" % h, align_bytes=64) for h in range(2)]
+        q_s = [sb.tile([P, D], U8, name="q_s%d" % h, align_bytes=64) for h in range(2)]
+        dec_c = [sb.tile([P, 2 * P], U32, name="dec_c%d" % j, align_bytes=64) for j in range(4)]
+        dec_s = [sb.tile([P, 2 * P], U8, name="dec_s%d" % j, align_bytes=64) for j in range(4)]
+
+        tr = {}
+        s1 = {}
+        s2 = {}
+
+        nc.scalar.dma_start(out=c_bf[:], in_=c.partition_broadcast(P))
+        nc.scalar.dma_start(out=b_bf[:], in_=b.partition_broadcast(P))
+        nc.scalar.dma_start(out=a_bf[:], in_=a.partition_broadcast(P))
+        nc.vector.memset(one1[:], 1.0)
+        nc.gpsimd.memset(bd_row[:], 0.0)
+        nc.gpsimd.memset(ones[:], 1.0)
+        make_identity(nc, ident[:])
+        nc.scalar.activation(out=junk[:], in_=one1[:], func=ACT.Ln)
+
+        def load_d(g):
+            nc.sync.dma_start(out=d_sb[g][:], in_=d_v[:, g, :])
+
+        def load_p(j):
+            nc.sync.dma_start(out=p_sb[j][:], in_=p_v[:, 2 * j : 2 * j + 2, :])
+
+        def load_q(j):
+            nc.sync.dma_start(out=q_sb[j][:], in_=q_v[:, 2 * j : 2 * j + 2, :])
+
+        load_d(0)
+        load_d(1)
+        nc.sync.dma_start(out=bd_row[0:1, :], in_=bd.rearrange("(o n) -> o n", o=1))
+        load_d(2)
+        nc.sync.dma_start(out=w_sb[:], in_=w_v)
+        load_p(0)
+        load_p(1)
+        load_d(3)
+        load_p(2)
+        load_p(3)
+        load_d(4)
+        load_q(0)
+        load_q(1)
+        load_d(5)
+        load_q(2)
+        load_q(3)
+        load_d(6)
+        load_d(7)
+
+        nc.vector.tensor_tensor(out=c_sq[:], in0=c_bf[:], in1=c_bf[:], op=ALU.mult)
+        nc.vector.tensor_scalar(out=c_fix[:], in0=c_sq[:], scalar1=0.0, scalar2=1e-18, op0=ALU.is_equal, op1=ALU.mult)
+        nc.vector.tensor_tensor(out=c_safe[:], in0=c_fix[:], in1=c_bf[:], op=ALU.add)
+        nc.vector.reciprocal(out=c_inv[:], in_=c_safe[:])
+        nc.vector.tensor_tensor(out=ratio[:], in0=c_inv[:], in1=b_bf[:], op=ALU.mult)
+
+        def copy_out(key, dst, src):
+            if key in V_COPIES:
+                nc.vector.tensor_copy(out=dst, in_=src)
+            else:
+                nc.scalar.copy(out=dst, in_=src)
+
+        def LN(g):
+            nc.scalar.activation(out=ln_sb[g][:], in_=d_sb[g][:], func=ACT.Ln)
+
+        def CB(g):
+            nc.vector.scalar_tensor_tensor(out=fx_sb[g][:], in0=ln_sb[g][:], scalar=ratio[:, 0:1], in1=d_sb[g][:], op0=ALU.mult, op1=ALU.add)
+
+        def EXP(g):
+            nc.scalar.activation(out=fx_sb[g][:], in_=fx_sb[g][:], func=ACT.Exp, scale=c_safe[:, 0:1])
+
+        def new_tr(key):
+            t = trp.tile([P, 4, P], F32, name="tr")
+            tr[key] = t
+            return t
+
+        def BIASMM():
+            t = new_tr("B")
+            nc.tensor.matmul(out=t[:].rearrange("p x s -> p (x s)"), lhsT=ones[:], rhs=bd_row[:], start=True, stop=True)
+
+        def BIASCP():
+            nc.vector.tensor_copy(
+                out=bias_bc[:].rearrange("p (u s e) -> p u s e", u=2, e=2),
+                in_=tr["B"][:].rearrange("p x s -> p (x s)").rearrange("p (s u e) -> p u s e", u=2, e=2),
+            )
+
+        def TW(u):
+            t = new_tr("W%d" % u)
+            words = w_sb[:].bitcast(F32)
+            for e in range(2):
+                for k in range(2):
+                    nc.tensor.transpose(t[:, 2 * e + k, :], words[:, 2 * u + e, k : D // 2 : 2], ident[:])
+
+        def CW(u):
+            copy_out(
+                "W%d" % u,
+                w_g[:].bitcast(F32)[:, D * u : D * (u + 1)].rearrange("p (s x) -> p s x", x=4),
+                tr["W%d" % u][:].rearrange("p x s -> p s x"),
+            )
+
+        def T2(key, src):
+            t = new_tr(key)
+            words = src[:].bitcast(F32)
+            for gl in range(2):
+                for k in range(2):
+                    nc.tensor.transpose(t[:, 2 * gl + k, :], words[:, gl, k : D // 2 : 2], ident[:])
+
+        def C2(key, dst_words):
+            copy_out(
+                key,
+                dst_words.rearrange("p (g r k) -> p g r k", g=2, k=2),
+                tr[key][:].rearrange("p (g k) r -> p g r k", g=2),
+            )
+
+        def TP(j):
+            T2("P%d" % j, p_sb[j])
+
+        def CP(j):
+            C2("P%d" % j, p_g[j // 2][:].bitcast(F32)[:, D * (j % 2) : D * (j % 2 + 1)])
+
+        def TQ(j):
+            T2("Q%d" % j, q_sb[j])
+
+        def CQ(j):
+            C2("Q%d" % j, q_g[j // 2][:].bitcast(F32)[:, D * (j % 2) : D * (j % 2 + 1)])
+
+        def TD(j):
+            t = new_tr("D%d" % j)
+            for gl in range(2):
+                words = dec_sb[2 * j + gl][:].bitcast(F32)
+                for u in range(2):
+                    nc.tensor.transpose(t[:, 2 * gl + u, :], words[:, P * u : P * (u + 1)], ident[:])
+
+        def CD(j):
+            C2("D%d" % j, dec_g[j][:].bitcast(F32))
+
+        def QZ(codes, scales, grouped):
+            nc.vector.quantize_mx(out=codes[:].bitcast(FP8X4), scales=scales[:], in_=grouped[:])
+
+        def M1(g):
+            t = s1p.tile([P, D], BANK_DT, name="s1")
+            s1[g] = t
+            cols = slice(P * (g % 4), P * (g % 4 + 1))
+            nc.tensor.matmul_mx(
+                out=t[:],
+                lhsT=p_c[g // 4][:, cols].bitcast(FP8X4),
+                lhsT_scale=p_s[g // 4][:, cols],
+                rhs=w_c[:].bitcast(FP8X4),
+                rhs_scale=w_s[:],
+                start=True,
+                stop=True,
+            )
+
+        def E1(g):
+            nc.vector.tensor_tensor(out=dec_sb[g][:], in0=s1[g][:], in1=bias_bc[:], op=ALU.add)
+
+        def M2(g, h):
+            t = s2p.tile([P, D], F32, name="s2")
+            s2[(g, h)] = t
+            cols = slice(P * (g % 2), P * (g % 2 + 1))
+            nc.tensor.matmul_mx(
+                out=t[:],
+                lhsT=dec_c[g // 2][:, cols].bitcast(FP8X4),
+                lhsT_scale=dec_s[g // 2][:, cols],
+                rhs=q_c[h][:].bitcast(FP8X4),
+                rhs_scale=q_s[h][:],
+                start=True,
+                stop=True,
+            )
+
+        def FIN(g, h):
+            cols = slice(D * h, D * (h + 1))
+            nc.vector.scalar_tensor_tensor(out=o_sb[g][:, cols], in0=s2[(g, h)][:], scalar=a_bf[:, 0:1], in1=fx_sb[g][:, cols], op0=ALU.mult, op1=ALU.mult)
+
+        def ST(g, h):
+            cols = slice(D * h, D * (h + 1))
+            nc.sync.dma_start(out=o_v[:, g, cols], in_=o_sb[g][:, cols])
+
+        LN(0)
+        CB(0)
+        BIASMM()
+        BIASCP()
+        LN(1)
+        CB(1)
+        LN(2)
+        CB(2)
+        TW(0)
+        TW(1)
+        CW(0)
+        CW(1)
+        QZ(w_c, w_s, w_g)
+        LN(3)
+        CB(3)
+        TP(0)
+        TP(1)
+        CP(0)
+        CP(1)
+        QZ(p_c[0], p_s[0], p_g[0])
+        TP(2)
+        TP(3)
+        M1(0)
+        E1(0)
+        M1(1)
+        E1(1)
+        LN(4)
+        CB(4)
+        M1(2)
+        E1(2)
+        M1(3)
+        E1(3)
+        CP(2)
+        CP(3)
+        QZ(p_c[1], p_s[1], p_g[1])
+        LN(5)
+        CB(5)
+        for j in range(4):
+            TQ(j)
+        M1(4)
+        E1(4)
+        M1(5)
+        E1(5)
+        CQ(0)
+        CQ(1)
+        QZ(q_c[0], q_s[0], q_g[0])
+        M1(6)
+        E1(6)
+        M1(7)
+        E1(7)
+        LN(6)
+        CB(6)
+        CQ(2)
+        CQ(3)
+        QZ(q_c[1], q_s[1], q_g[1])
+        LN(7)
+        CB(7)
+        for j in range(4):
+            TD(j)
+        for j in range(4):
+            CD(j)
+        for j in range(4):
+            QZ(dec_c[j], dec_s[j], dec_g[j])
+        for g in range(G):
+            M2(g, 0)
+            M2(g, 1)
+            EXP(g)
+            for h in range(2):
+                FIN(g, h)
+                ST(g, h)

@@ -18,7 +18,8 @@ G = 8
 N = 1024
 D = 512
 BANK_DT = F32
-V_COPIES = ()
+G_TILES = (6, 7)
+V_COPIES = ("D1", "D2", "D3")
 
 
 def tile_gglr_pb_kernel(tc, p_last, q_last, distance_matrix, Wd, bd, a, b, c, out):
@@ -29,6 +30,8 @@ def tile_gglr_pb_kernel(tc, p_last, q_last, distance_matrix, Wd, bd, a, b, c, ou
         trp = ctx.enter_context(tc.psum_pool(name="trp", bufs=3))
         s1p = ctx.enter_context(tc.psum_pool(name="s1p", bufs=2))
         s2p = ctx.enter_context(tc.psum_pool(name="s2p", bufs=3))
+
+        scratch = s2p.tile([P, D], F32, name="s2")
 
         d_v = distance_matrix.rearrange("(r g) n -> r g n", g=G)
         o_v = out.rearrange("(r g) n -> r g n", g=G)
@@ -46,6 +49,7 @@ def tile_gglr_pb_kernel(tc, p_last, q_last, distance_matrix, Wd, bd, a, b, c, ou
         c_safe = sb.tile([P, 1], F32, name="c_safe")
         c_inv = sb.tile([P, 1], F32, name="c_inv")
         ratio = sb.tile([P, 1], F32, name="ratio")
+        ratio_g = sb.tile([P, 1], F32, name="ratio_g")
         ident = sb.tile([P, P], F32, name="ident")
         ones = sb.tile([P, P], BF16, name="ones")
         bd_row = sb.tile([P, D], BF16, name="bd_row")
@@ -54,6 +58,9 @@ def tile_gglr_pb_kernel(tc, p_last, q_last, distance_matrix, Wd, bd, a, b, c, ou
         d_sb = [sb.tile([P, N], BF16, name="d_sb%d" % g) for g in range(G)]
         ln_sb = [sb.tile([P, N], F32, name="ln_sb%d" % g) for g in range(G)]
         fx_sb = [sb.tile([P, N], F32, name="fx_sb%d" % g) for g in range(G)]
+        rl_sb = {}
+        for g in G_TILES:
+            rl_sb[g] = sb.tile([P, N], F32, name="rl_sb%d" % g)
         o_sb = [sb.tile([P, N], F32, name="o_sb%d" % g) for g in range(G)]
 
         w_sb = sb.tile([P, 4, D], BF16, name="w_sb")
@@ -86,8 +93,8 @@ def tile_gglr_pb_kernel(tc, p_last, q_last, distance_matrix, Wd, bd, a, b, c, ou
         make_identity(nc, ident[:])
         nc.scalar.activation(out=junk[:], in_=one1[:], func=ACT.Ln)
 
-        def load_d(g):
-            nc.sync.dma_start(out=d_sb[g][:], in_=d_v[:, g, :])
+        def load_d(g, lo=0, hi=N):
+            nc.sync.dma_start(out=d_sb[g][:, lo:hi], in_=d_v[:, g, lo:hi])
 
         def load_p(j):
             nc.sync.dma_start(out=p_sb[j][:], in_=p_v[:, 2 * j : 2 * j + 2, :])
@@ -95,23 +102,24 @@ def tile_gglr_pb_kernel(tc, p_last, q_last, distance_matrix, Wd, bd, a, b, c, ou
         def load_q(j):
             nc.sync.dma_start(out=q_sb[j][:], in_=q_v[:, 2 * j : 2 * j + 2, :])
 
-        load_d(0)
+        load_d(0, 0, D)
+        load_d(0, D, N)
         load_d(1)
         nc.sync.dma_start(out=bd_row[0:1, :], in_=bd.rearrange("(o n) -> o n", o=1))
         load_d(2)
         nc.sync.dma_start(out=w_sb[:], in_=w_v)
         load_p(0)
-        load_p(1)
         load_d(3)
+        load_p(1)
+        load_d(4)
         load_p(2)
         load_p(3)
-        load_d(4)
+        load_d(5)
         load_q(0)
         load_q(1)
-        load_d(5)
+        load_d(6)
         load_q(2)
         load_q(3)
-        load_d(6)
         load_d(7)
 
         nc.vector.tensor_tensor(out=c_sq[:], in0=c_bf[:], in1=c_bf[:], op=ALU.mult)
@@ -126,14 +134,25 @@ def tile_gglr_pb_kernel(tc, p_last, q_last, distance_matrix, Wd, bd, a, b, c, ou
             else:
                 nc.scalar.copy(out=dst, in_=src)
 
-        def LN(g):
-            nc.scalar.activation(out=ln_sb[g][:], in_=d_sb[g][:], func=ACT.Ln)
+        def LN(g, lo=0, hi=N):
+            nc.scalar.activation(out=ln_sb[g][:, lo:hi], in_=d_sb[g][:, lo:hi], func=ACT.Ln)
 
-        def CB(g):
-            nc.vector.scalar_tensor_tensor(out=fx_sb[g][:], in0=ln_sb[g][:], scalar=ratio[:, 0:1], in1=d_sb[g][:], op0=ALU.mult, op1=ALU.add)
+        def CB(g, lo=0, hi=N):
+            nc.vector.scalar_tensor_tensor(out=fx_sb[g][:, lo:hi], in0=ln_sb[g][:, lo:hi], scalar=ratio[:, 0:1], in1=d_sb[g][:, lo:hi], op0=ALU.mult, op1=ALU.add)
 
-        def EXP(g):
-            nc.scalar.activation(out=fx_sb[g][:], in_=fx_sb[g][:], func=ACT.Exp, scale=c_safe[:, 0:1])
+        def WARM(n):
+            for i in range(n):
+                nc.tensor.matmul(out=scratch[:, 0:P], lhsT=ident[:], rhs=ident[:], start=True, stop=True)
+
+        def GATE():
+            nc.vector.tensor_copy(out=ratio_g[:], in_=ratio[:])
+
+        def GC(g, lo=0, hi=N):
+            nc.gpsimd.tensor_scalar(out=rl_sb[g][:, lo:hi], in0=ln_sb[g][:, lo:hi], scalar1=ratio_g[:, 0:1], scalar2=0.0, op0=ALU.mult, op1=ALU.add)
+            nc.gpsimd.tensor_tensor(out=fx_sb[g][:, lo:hi], in0=rl_sb[g][:, lo:hi], in1=d_sb[g][:, lo:hi], op=ALU.add)
+
+        def EXP(g, lo=0, hi=N):
+            nc.scalar.activation(out=fx_sb[g][:, lo:hi], in_=fx_sb[g][:, lo:hi], func=ACT.Exp, scale=c_safe[:, 0:1])
 
         def new_tr(key):
             t = trp.tile([P, 4, P], F32, name="tr")
@@ -234,15 +253,17 @@ def tile_gglr_pb_kernel(tc, p_last, q_last, distance_matrix, Wd, bd, a, b, c, ou
                 stop=True,
             )
 
-        def FIN(g, h):
-            cols = slice(D * h, D * (h + 1))
-            nc.vector.scalar_tensor_tensor(out=o_sb[g][:, cols], in0=s2[(g, h)][:], scalar=a_bf[:, 0:1], in1=fx_sb[g][:, cols], op0=ALU.mult, op1=ALU.mult)
+        def FIN(g, h, lo=0, hi=D):
+            cols = slice(D * h + lo, D * h + hi)
+            nc.vector.scalar_tensor_tensor(out=o_sb[g][:, cols], in0=s2[(g, h)][:, lo:hi], scalar=a_bf[:, 0:1], in1=fx_sb[g][:, cols], op0=ALU.mult, op1=ALU.mult)
 
-        def ST(g, h):
-            cols = slice(D * h, D * (h + 1))
+        def ST(g, h, lo=0, hi=D):
+            cols = slice(D * h + lo, D * h + hi)
             nc.sync.dma_start(out=o_v[:, g, cols], in_=o_sb[g][:, cols])
 
-        LN(0)
+        WARM(6)
+        LN(0, 0, D)
+        LN(0, D, N)
         CB(0)
         BIASMM()
         BIASCP()
@@ -252,6 +273,7 @@ def tile_gglr_pb_kernel(tc, p_last, q_last, distance_matrix, Wd, bd, a, b, c, ou
         CB(2)
         TW(0)
         TW(1)
+        WARM(1)
         CW(0)
         CW(1)
         QZ(w_c, w_s, w_g)
@@ -259,11 +281,13 @@ def tile_gglr_pb_kernel(tc, p_last, q_last, distance_matrix, Wd, bd, a, b, c, ou
         CB(3)
         TP(0)
         TP(1)
+        WARM(2)
         CP(0)
         CP(1)
         QZ(p_c[0], p_s[0], p_g[0])
         TP(2)
         TP(3)
+        WARM(2)
         M1(0)
         E1(0)
         M1(1)
@@ -279,8 +303,12 @@ def tile_gglr_pb_kernel(tc, p_last, q_last, distance_matrix, Wd, bd, a, b, c, ou
         QZ(p_c[1], p_s[1], p_g[1])
         LN(5)
         CB(5)
-        for j in range(4):
-            TQ(j)
+        TQ(0)
+        TQ(1)
+        WARM(1)
+        TQ(2)
+        TQ(3)
+        WARM(1)
         M1(4)
         E1(4)
         M1(5)
@@ -293,22 +321,35 @@ def tile_gglr_pb_kernel(tc, p_last, q_last, distance_matrix, Wd, bd, a, b, c, ou
         M1(7)
         E1(7)
         LN(6)
-        CB(6)
         CQ(2)
         CQ(3)
         QZ(q_c[1], q_s[1], q_g[1])
         LN(7)
-        CB(7)
+        CB(7, 0, D)
         for j in range(4):
             TD(j)
         for j in range(4):
             CD(j)
         for j in range(4):
             QZ(dec_c[j], dec_s[j], dec_g[j])
+        GATE()
+        GC(6)
+        GC(7, D, N)
         for g in range(G):
             M2(g, 0)
             M2(g, 1)
-            EXP(g)
-            for h in range(2):
-                FIN(g, h)
-                ST(g, h)
+            if g == 0:
+                EXP(g, 0, D)
+                EXP(g, D, N)
+            else:
+                EXP(g)
+            FIN(g, 0)
+            ST(g, 0)
+            if g < G - 1:
+                FIN(g, 1)
+                ST(g, 1)
+            else:
+                FIN(g, 1, 0, D // 2)
+                ST(g, 1, 0, D // 2)
+                FIN(g, 1, D // 2, D)
+                ST(g, 1, D // 2, D)

from contextlib import ExitStack

import concourse.mybir as mybir
from concourse.masks import make_identity

FLOPS = 2 * 1024 * 512 * 512 + 2 * 1024 * 1024 * 512

F32 = mybir.dt.float32
BF16 = mybir.dt.bfloat16
U32 = mybir.dt.uint32
U8 = mybir.dt.uint8
FP8X4 = mybir.dt.float8_e4m3fn_x4
ACT = mybir.ActivationFunctionType
ALU = mybir.AluOpType

P = 128
G = 8
N = 1024
D = 512
BANK_DT = F32
G_TILES = (6, 7)
V_COPIES = ("D1", "D2", "D3")


def tile_gglr_pb_kernel(tc, p_last, q_last, distance_matrix, Wd, bd, a, b, c, out):
    nc = tc.nc
    with ExitStack() as ctx:
        ctx.enter_context(tc.manual_schedule())
        sb = ctx.enter_context(tc.tile_pool(name="sb", bufs=1))
        trp = ctx.enter_context(tc.psum_pool(name="trp", bufs=3))
        s1p = ctx.enter_context(tc.psum_pool(name="s1p", bufs=2))
        s2p = ctx.enter_context(tc.psum_pool(name="s2p", bufs=3))

        scratch = s2p.tile([P, D], F32, name="s2")

        d_v = distance_matrix.rearrange("(r g) n -> r g n", g=G)
        o_v = out.rearrange("(r g) n -> r g n", g=G)
        p_v = p_last.rearrange("(r g) k -> r g k", g=G)
        q_v = q_last.rearrange("(h r) k -> r h k", r=P)
        w_v = Wd.rearrange("(s q) k -> s q k", q=4)

        c_bf = sb.tile([P, 1], BF16, name="c_bf")
        b_bf = sb.tile([P, 1], BF16, name="b_bf")
        a_bf = sb.tile([P, 1], BF16, name="a_bf")
        one1 = sb.tile([P, 1], F32, name="one1")
        junk = sb.tile([P, 1], F32, name="junk")
        c_sq = sb.tile([P, 1], F32, name="c_sq")
        c_fix = sb.tile([P, 1], F32, name="c_fix")
        c_safe = sb.tile([P, 1], F32, name="c_safe")
        c_inv = sb.tile([P, 1], F32, name="c_inv")
        ratio = sb.tile([P, 1], F32, name="ratio")
        ratio_g = sb.tile([P, 1], F32, name="ratio_g")
        ident = sb.tile([P, P], F32, name="ident")
        ones = sb.tile([P, P], BF16, name="ones")
        bd_row = sb.tile([P, D], BF16, name="bd_row")
        bias_bc = sb.tile([P, D], BF16, name="bias_bc")

        d_sb = [sb.tile([P, N], BF16, name="d_sb%d" % g) for g in range(G)]
        ln_sb = [sb.tile([P, N], F32, name="ln_sb%d" % g) for g in range(G)]
        fx_sb = [sb.tile([P, N], F32, name="fx_sb%d" % g) for g in range(G)]
        rl_sb = {}
        for g in G_TILES:
            rl_sb[g] = sb.tile([P, N], F32, name="rl_sb%d" % g)
        o_sb = [sb.tile([P, N], F32, name="o_sb%d" % g) for g in range(G)]

        w_sb = sb.tile([P, 4, D], BF16, name="w_sb")
        p_sb = [sb.tile([P, 2, D], BF16, name="p_sb%d" % j) for j in range(4)]
        q_sb = [sb.tile([P, 2, D], BF16, name="q_sb%d" % j) for j in range(4)]
        w_g = sb.tile([P, 4 * D], BF16, name="w_g", align_bytes=64)
        p_g = [sb.tile([P, 4 * D], BF16, name="p_g%d" % h, align_bytes=64) for h in range(2)]
        q_g = [sb.tile([P, 4 * D], BF16, name="q_g%d" % h, align_bytes=64) for h in range(2)]
        dec_sb = [sb.tile([P, D], BF16, name="dec_sb%d" % g) for g in range(G)]
        dec_g = [sb.tile([P, 2 * D], BF16, name="dec_g%d" % j, align_bytes=64) for j in range(4)]
        w_c = sb.tile([P, D], U32, name="w_c", align_bytes=64)
        w_s = sb.tile([P, D], U8, name="w_s", align_bytes=64)
        p_c = [sb.tile([P, D], U32, name="p_c%d" % h, align_bytes=64) for h in range(2)]
        p_s = [sb.tile([P, D], U8, name="p_s%d" % h, align_bytes=64) for h in range(2)]
        q_c = [sb.tile([P, D], U32, name="q_c%d" % h, align_bytes=64) for h in range(2)]
        q_s = [sb.tile([P, D], U8, name="q_s%d" % h, align_bytes=64) for h in range(2)]
        dec_c = [sb.tile([P, 2 * P], U32, name="dec_c%d" % j, align_bytes=64) for j in range(4)]
        dec_s = [sb.tile([P, 2 * P], U8, name="dec_s%d" % j, align_bytes=64) for j in range(4)]

        tr = {}
        s1 = {}
        s2 = {}

        nc.scalar.dma_start(out=c_bf[:], in_=c.partition_broadcast(P))
        nc.scalar.dma_start(out=b_bf[:], in_=b.partition_broadcast(P))
        nc.scalar.dma_start(out=a_bf[:], in_=a.partition_broadcast(P))
        nc.vector.memset(one1[:], 1.0)
        nc.gpsimd.memset(bd_row[:], 0.0)
        nc.gpsimd.memset(ones[:], 1.0)
        make_identity(nc, ident[:])
        nc.scalar.activation(out=junk[:], in_=one1[:], func=ACT.Ln)

        def load_d(g, lo=0, hi=N):
            nc.sync.dma_start(out=d_sb[g][:, lo:hi], in_=d_v[:, g, lo:hi])

        def load_p(j):
            nc.sync.dma_start(out=p_sb[j][:], in_=p_v[:, 2 * j : 2 * j + 2, :])

        def load_q(j):
            nc.sync.dma_start(out=q_sb[j][:], in_=q_v[:, 2 * j : 2 * j + 2, :])

        load_d(0, 0, D)
        load_d(0, D, N)
        load_d(1)
        nc.sync.dma_start(out=bd_row[0:1, :], in_=bd.rearrange("(o n) -> o n", o=1))
        load_d(2)
        nc.sync.dma_start(out=w_sb[:], in_=w_v)
        load_p(0)
        load_d(3)
        load_p(1)
        load_d(4)
        load_p(2)
        load_p(3)
        load_d(5)
        load_q(0)
        load_q(1)
        load_d(6)
        load_q(2)
        load_q(3)
        load_d(7)

        nc.vector.tensor_tensor(out=c_sq[:], in0=c_bf[:], in1=c_bf[:], op=ALU.mult)
        nc.vector.tensor_scalar(out=c_fix[:], in0=c_sq[:], scalar1=0.0, scalar2=1e-18, op0=ALU.is_equal, op1=ALU.mult)
        nc.vector.tensor_tensor(out=c_safe[:], in0=c_fix[:], in1=c_bf[:], op=ALU.add)
        nc.vector.reciprocal(out=c_inv[:], in_=c_safe[:])
        nc.vector.tensor_tensor(out=ratio[:], in0=c_inv[:], in1=b_bf[:], op=ALU.mult)

        def copy_out(key, dst, src):
            if key in V_COPIES:
                nc.vector.tensor_copy(out=dst, in_=src)
            else:
                nc.scalar.copy(out=dst, in_=src)

        def LN(g, lo=0, hi=N):
            nc.scalar.activation(out=ln_sb[g][:, lo:hi], in_=d_sb[g][:, lo:hi], func=ACT.Ln)

        def CB(g, lo=0, hi=N):
            nc.vector.scalar_tensor_tensor(out=fx_sb[g][:, lo:hi], in0=ln_sb[g][:, lo:hi], scalar=ratio[:, 0:1], in1=d_sb[g][:, lo:hi], op0=ALU.mult, op1=ALU.add)

        def WARM(n):
            for i in range(n):
                nc.tensor.matmul(out=scratch[:, 0:P], lhsT=ident[:], rhs=ident[:], start=True, stop=True)

        def GATE():
            nc.vector.tensor_copy(out=ratio_g[:], in_=ratio[:])

        def GC(g, lo=0, hi=N):
            nc.gpsimd.tensor_scalar(out=rl_sb[g][:, lo:hi], in0=ln_sb[g][:, lo:hi], scalar1=ratio_g[:, 0:1], scalar2=0.0, op0=ALU.mult, op1=ALU.add)
            nc.gpsimd.tensor_tensor(out=fx_sb[g][:, lo:hi], in0=rl_sb[g][:, lo:hi], in1=d_sb[g][:, lo:hi], op=ALU.add)

        def EXP(g, lo=0, hi=N):
            nc.scalar.activation(out=fx_sb[g][:, lo:hi], in_=fx_sb[g][:, lo:hi], func=ACT.Exp, scale=c_safe[:, 0:1])

        def new_tr(key):
            t = trp.tile([P, 4, P], F32, name="tr")
            tr[key] = t
            return t

        def BIASMM():
            t = new_tr("B")
            nc.tensor.matmul(out=t[:].rearrange("p x s -> p (x s)"), lhsT=ones[:], rhs=bd_row[:], start=True, stop=True)

        def BIASCP():
            nc.vector.tensor_copy(
                out=bias_bc[:].rearrange("p (u s e) -> p u s e", u=2, e=2),
                in_=tr["B"][:].rearrange("p x s -> p (x s)").rearrange("p (s u e) -> p u s e", u=2, e=2),
            )

        def TW(u):
            t = new_tr("W%d" % u)
            words = w_sb[:].bitcast(F32)
            for e in range(2):
                for k in range(2):
                    nc.tensor.transpose(t[:, 2 * e + k, :], words[:, 2 * u + e, k : D // 2 : 2], ident[:])

        def CW(u):
            copy_out(
                "W%d" % u,
                w_g[:].bitcast(F32)[:, D * u : D * (u + 1)].rearrange("p (s x) -> p s x", x=4),
                tr["W%d" % u][:].rearrange("p x s -> p s x"),
            )

        def T2(key, src):
            t = new_tr(key)
            words = src[:].bitcast(F32)
            for gl in range(2):
                for k in range(2):
                    nc.tensor.transpose(t[:, 2 * gl + k, :], words[:, gl, k : D // 2 : 2], ident[:])

        def C2(key, dst_words):
            copy_out(
                key,
                dst_words.rearrange("p (g r k) -> p g r k", g=2, k=2),
                tr[key][:].rearrange("p (g k) r -> p g r k", g=2),
            )

        def TP(j):
            T2("P%d" % j, p_sb[j])

        def CP(j):
            C2("P%d" % j, p_g[j // 2][:].bitcast(F32)[:, D * (j % 2) : D * (j % 2 + 1)])

        def TQ(j):
            T2("Q%d" % j, q_sb[j])

        def CQ(j):
            C2("Q%d" % j, q_g[j // 2][:].bitcast(F32)[:, D * (j % 2) : D * (j % 2 + 1)])

        def TD(j):
            t = new_tr("D%d" % j)
            for gl in range(2):
                words = dec_sb[2 * j + gl][:].bitcast(F32)
                for u in range(2):
                    nc.tensor.transpose(t[:, 2 * gl + u, :], words[:, P * u : P * (u + 1)], ident[:])

        def CD(j):
            C2("D%d" % j, dec_g[j][:].bitcast(F32))

        def QZ(codes, scales, grouped):
            nc.vector.quantize_mx(out=codes[:].bitcast(FP8X4), scales=scales[:], in_=grouped[:])

        def M1(g):
            t = s1p.tile([P, D], BANK_DT, name="s1")
            s1[g] = t
            cols = slice(P * (g % 4), P * (g % 4 + 1))
            nc.tensor.matmul_mx(
                out=t[:],
                lhsT=p_c[g // 4][:, cols].bitcast(FP8X4),
                lhsT_scale=p_s[g // 4][:, cols],
                rhs=w_c[:].bitcast(FP8X4),
                rhs_scale=w_s[:],
                start=True,
                stop=True,
            )

        def E1(g):
            nc.vector.tensor_tensor(out=dec_sb[g][:], in0=s1[g][:], in1=bias_bc[:], op=ALU.add)

        def M2(g, h):
            t = s2p.tile([P, D], F32, name="s2")
            s2[(g, h)] = t
            cols = slice(P * (g % 2), P * (g % 2 + 1))
            nc.tensor.matmul_mx(
                out=t[:],
                lhsT=dec_c[g // 2][:, cols].bitcast(FP8X4),
                lhsT_scale=dec_s[g // 2][:, cols],
                rhs=q_c[h][:].bitcast(FP8X4),
                rhs_scale=q_s[h][:],
                start=True,
                stop=True,
            )

        def FIN(g, h, lo=0, hi=D):
            cols = slice(D * h + lo, D * h + hi)
            nc.vector.scalar_tensor_tensor(out=o_sb[g][:, cols], in0=s2[(g, h)][:, lo:hi], scalar=a_bf[:, 0:1], in1=fx_sb[g][:, cols], op0=ALU.mult, op1=ALU.mult)

        def ST(g, h, lo=0, hi=D):
            cols = slice(D * h + lo, D * h + hi)
            nc.sync.dma_start(out=o_v[:, g, cols], in_=o_sb[g][:, cols])

        WARM(6)
        LN(0, 0, D)
        LN(0, D, N)
        CB(0)
        BIASMM()
        BIASCP()
        LN(1)
        CB(1)
        LN(2)
        CB(2)
        TW(0)
        TW(1)
        WARM(1)
        CW(0)
        CW(1)
        QZ(w_c, w_s, w_g)
        LN(3)
        CB(3)
        TP(0)
        TP(1)
        WARM(2)
        CP(0)
        CP(1)
        QZ(p_c[0], p_s[0], p_g[0])
        TP(2)
        TP(3)
        WARM(2)
        M1(0)
        E1(0)
        M1(1)
        E1(1)
        LN(4)
        CB(4)
        M1(2)
        E1(2)
        M1(3)
        E1(3)
        CP(2)
        CP(3)
        QZ(p_c[1], p_s[1], p_g[1])
        LN(5)
        CB(5)
        TQ(0)
        TQ(1)
        WARM(1)
        TQ(2)
        TQ(3)
        WARM(1)
        M1(4)
        E1(4)
        M1(5)
        E1(5)
        CQ(0)
        CQ(1)
        QZ(q_c[0], q_s[0], q_g[0])
        M1(6)
        E1(6)
        M1(7)
        E1(7)
        LN(6)
        CQ(2)
        CQ(3)
        QZ(q_c[1], q_s[1], q_g[1])
        LN(7)
        CB(7, 0, D)
        for j in range(4):
            TD(j)
        for j in range(4):
            CD(j)
        for j in range(4):
            QZ(dec_c[j], dec_s[j], dec_g[j])
        GATE()
        GC(6)
        GC(7, D, N)
        for g in range(G):
            M2(g, 0)
            M2(g, 1)
            if g == 0:
                EXP(g, 0, D)
                EXP(g, D, N)
            else:
                EXP(g)
            FIN(g, 0)
            ST(g, 0)
            if g < G - 1:
                FIN(g, 1)
                ST(g, 1)
            else:
                FIN(g, 1, 0, D // 2)
                ST(g, 1, 0, D // 2)
                FIN(g, 1, D // 2, D)
                ST(g, 1, D // 2, D)
